import numpy as np
import ml_dtypes


def mxq(x, axis, fmt="e4m3"):
    dtype, down = {"e4m3": (ml_dtypes.float8_e4m3fn, 7), "e5m2": (ml_dtypes.float8_e5m2, 14)}[fmt]
    v = np.moveaxis(np.asarray(x, np.float32).astype(ml_dtypes.bfloat16).astype(np.float64), axis, -1)
    blocks = v.reshape(v.shape[:-1] + (-1, 32))
    amax = np.abs(blocks).max(-1, keepdims=True)
    byte = np.maximum(np.where(amax > 0, np.frexp(amax)[1] - 1 + 127, 0) - down, 1)
    scale = np.exp2(byte - 127.0)
    codes = (blocks / scale).astype(np.float32).astype(dtype).astype(np.float64)
    return np.moveaxis((codes * scale).reshape(v.shape), -1, axis)


WIDE = False


def mx_kscale(k):
    if not WIDE:
        return np.ones(k)
    levels = np.array([10, -10, 5, -5, 0])
    a = np.random.permutation(np.resize(levels, k // 512 * 4)).reshape(k // 512, 4)
    idx = np.arange(k)
    return np.exp2(a[idx // 512, idx % 128 // 32])


BF16 = ml_dtypes.bfloat16


def bf(x):
    return np.asarray(x, np.float32).astype(BF16)


def f64(x):
    return np.asarray(x).astype(np.float64)


B, T, D, DI = 4, 1024, 512, 512
ROPE_BASE = 10000.0


def rotate_half(v):
    h = v.shape[-1] // 2
    return np.concatenate([-v[..., h:], v[..., :h]], axis=-1)


def justnorm(v):
    return v / np.sqrt((v * v).sum(-1, keepdims=True))


def setup_inputs():
    s = mx_kscale(D)
    x = np.random.standard_normal((B, T, D)) * np.exp(0.5 * np.random.standard_normal((B, T, 1)))
    w = justnorm(np.random.uniform(-1.0, 1.0, (2 * DI, D)))
    inv_freq = 1.0 / ROPE_BASE ** (np.arange(0, DI, 2) / DI)
    pos = np.random.randint(0, T) + np.arange(T)
    freqs = pos[:, None] * inv_freq[None, :]
    emb = np.concatenate([freqs, freqs], axis=-1)
    return {"input_vecs": bf(x * s), "qk_w": bf(w / s),
            "sqk": bf(3.0 * (1.0 + 0.2 * np.random.standard_normal(DI)) / np.sqrt(D)),
            "cos": bf(np.cos(emb)), "sin": bf(np.sin(emb))}


def reference(input_vecs, qk_w, sqk, cos, sin):
    qk = mxq(f64(input_vecs), 2, "e4m3") @ mxq(f64(qk_w), 1, "e4m3").T
    q, k = np.split(qk, 2, axis=-1)
    c, sn = f64(cos), f64(sin)
    q = q * c + rotate_half(q) * sn
    k = k * c + rotate_half(k) * sn
    sqk_eff = f64(sqk) * np.sqrt(D)
    return justnorm(q) * sqk_eff, justnorm(k) * sqk_eff

@@ -1,0 +1,169 @@
+from contextlib import ExitStack
+
+import concourse.mybir as mybir
+from concourse.masks import make_identity
+
+F32 = mybir.dt.float32
+BF16 = mybir.dt.bfloat16
+U32 = mybir.dt.uint32
+U8 = mybir.dt.uint8
+FP8X4 = mybir.dt.float8_e4m3fn_x4
+ACT = mybir.ActivationFunctionType
+ALU = mybir.AluOpType
+
+P = 128
+B, T, D, DI = 4, 1024, 512, 512
+NT = T // P
+NPAIR = NT // 2
+NJ = DI // P
+GT = 2 * P
+FLOPS = 2 * B * T * D * 2 * DI
+
+
+def tile_attentionhead_pa_t_kernel(tc, input_vecs, qk_w, sqk, cos, sin, out_0, out_1):
+    nc = tc.nc
+    x_v = input_vecs.rearrange("b (p n) k -> b p n k", n=NT)
+    w_v = qk_w.rearrange("(r p) k -> p r k", p=P)
+    cos_v = cos.rearrange("(p n) c -> p n c", n=NT)
+    sin_v = sin.rearrange("(p n) c -> p n c", n=NT)
+    o_v = [o.rearrange("b (p n) c -> b p n c", n=NT) for o in (out_0, out_1)]
+
+    with ExitStack() as ctx:
+        const = ctx.enter_context(tc.tile_pool(name="const", bufs=1))
+        stage = ctx.enter_context(tc.tile_pool(name="stage", bufs=3))
+        prods = ctx.enter_context(tc.tile_pool(name="prods", bufs=3))
+        outs = ctx.enter_context(tc.tile_pool(name="outs", bufs=4))
+        small = ctx.enter_context(tc.tile_pool(name="small", bufs=4))
+        psum = ctx.enter_context(tc.psum_pool(name="psum", bufs=4))
+
+        ident_f = const.tile([P, P], F32, name="ident_f")
+        make_identity(nc, ident_f[:])
+        ident_b = const.tile([P, P], BF16, name="ident_b")
+        make_identity(nc, ident_b[:])
+        one = const.tile([P, 1], F32, name="one")
+        nc.vector.memset(one[:], 1.0)
+        warm = const.tile([P, 1], F32, name="warm")
+        nc.scalar.activation(out=warm[:], in_=one[:], func=ACT.Sqrt)
+
+        xr = [const.tile([P, NT, D], BF16, name="xr%d" % b) for b in range(B)]
+        wr = const.tile([P, 2 * NJ, D], BF16, name="wr")
+        cr = const.tile([P, NT, DI], BF16, name="cr")
+        sr = const.tile([P, NT, DI], BF16, name="sr")
+        gb = const.tile([P, DI], BF16, name="gb")
+        xc = const.tile([P, B * T], U32, name="xc", align_bytes=64)
+        xs = const.tile([P, B * T], U8, name="xs", align_bytes=64)
+        wc = const.tile([P, 2 * DI], U32, name="wc", align_bytes=64)
+        ws = const.tile([P, 2 * DI], U8, name="ws", align_bytes=64)
+        ct = const.tile([P, NJ, NPAIR, GT], BF16, name="ct")
+        st = const.tile([P, NJ, NPAIR, GT], BF16, name="st")
+
+        nc.sync.dma_start(out=wr[:, 0:NJ, :], in_=w_v[:, 0:NJ, :])
+        nc.sync.dma_start(out=xr[0][:, 0:2, :], in_=x_v[0][:, 0:2, :])
+        nc.sync.dma_start(out=cr[:, 0:2, :], in_=cos_v[:, 0:2, :])
+        nc.sync.dma_start(out=sr[:, 0:2, :], in_=sin_v[:, 0:2, :])
+        nc.sync.dma_start(out=wr[:, NJ : 2 * NJ, :], in_=w_v[:, NJ : 2 * NJ, :])
+        nc.sync.dma_start(out=xr[0][:, 2:NT, :], in_=x_v[0][:, 2:NT, :])
+        nc.sync.dma_start(out=gb[:], in_=sqk.partition_broadcast(P))
+        nc.sync.dma_start(out=cr[:, 2:NT, :], in_=cos_v[:, 2:NT, :])
+        nc.sync.dma_start(out=sr[:, 2:NT, :], in_=sin_v[:, 2:NT, :])
+        for b in range(1, B):
+            nc.sync.dma_start(out=xr[b][:], in_=x_v[b])
+
+        def quantise_rows(rows, codes, scales, tag):
+            grouped = stage.tile([P, len(rows) * P * 4], BF16, tag=tag, name="grouped", align_bytes=64)
+            gw = grouped[:].bitcast(F32).rearrange("p (m i r u) -> p m i r u", i=2, r=P, u=2)
+            for m in range(len(rows) // 2):
+                pt = psum.tile([P, 2, 2, P], F32, tag="tp", name="pt")
+                for i in range(2):
+                    words = rows[2 * m + i].bitcast(F32)
+                    for u in range(2):
+                        nc.tensor.transpose(pt[:, i, u, :], words[:, u * P : (u + 1) * P], ident_f[:])
+                nc.vector.tensor_copy(out=gw[:, m], in_=pt[:].rearrange("p i u r -> p i r u"))
+            nc.vector.quantize_mx(out=codes.bitcast(FP8X4), scales=scales, in_=grouped[:])
+
+        def prep_w(h):
+            cols = slice(h * DI, (h + 1) * DI)
+            quantise_rows([wr[:, h * NJ + j, :] for j in range(NJ)], wc[:, cols], ws[:, cols], "wg")
+
+        def prep_x(s):
+            b, q = divmod(s, NPAIR)
+            cols = slice(s * GT, (s + 1) * GT)
+            quantise_rows([xr[b][:, 2 * q + i, :] for i in range(2)], xc[:, cols], xs[:, cols], "xg")
+
+        def prep_tab(q):
+            for raw, tab, negate in ((cr, ct, False), (sr, st, True)):
+                ptb = psum.tile([P, NJ, GT], BF16, tag="tp", name="ptb")
+                for j in range(NJ):
+                    for i in range(2):
+                        nc.tensor.transpose(
+                            ptb[:, j, i * P : (i + 1) * P], raw[:, 2 * q + i, j * P : (j + 1) * P], ident_b[:]
+                        )
+                if negate:
+                    nc.scalar.mul(out=tab[:, 0:2, q, :], in_=ptb[:, 0:2, :], mul=-1.0)
+                    nc.scalar.copy(out=tab[:, 2:4, q, :], in_=ptb[:, 2:4, :])
+                else:
+                    nc.scalar.copy(out=tab[:, :, q, :], in_=ptb[:])
+
+        def group(s, h):
+            b, q = divmod(s, NPAIR)
+            tok = slice(s * GT, (s + 1) * GT)
+            banks = []
+            for half in range(2):
+                u = psum.tile([P, 2, GT], F32, tag="mx", name="u")
+                banks.append(u)
+                for jj in range(2):
+                    c0 = h * DI + (2 * half + jj) * P
+                    nc.tensor.matmul_mx(
+                        out=u[:, jj, :],
+                        lhsT=wc[:, c0 : c0 + P].bitcast(FP8X4),
+                        lhsT_scale=ws[:, c0 : c0 + P],
+                        rhs=xc[:, tok].bitcast(FP8X4),
+                        rhs_scale=xs[:, tok],
+                        start=True,
+                        stop=True,
+                    )
+            a_t = prods.tile([P, NJ, GT], F32, tag="a", name="a_t")
+            b_t = prods.tile([P, NJ, GT], F32, tag="b", name="b_t")
+            for half in range(2):
+                js = slice(2 * half, 2 * half + 2)
+                nc.vector.tensor_tensor(out=a_t[:, js, :], in0=banks[half][:], in1=ct[:, js, q, :], op=ALU.mult)
+                nc.vector.tensor_tensor(out=b_t[:, js, :], in0=banks[1 - half][:], in1=st[:, js, q, :], op=ALU.mult)
+            ssq = small.tile([P, 2], F32, tag="ssq", name="ssq")
+            rbs = []
+            for i in range(2):
+                rb = psum.tile([P, DI], F32, tag="tp", name="rb")
+                rbs.append(rb)
+                ts = slice(i * P, (i + 1) * P)
+                for j in range(NJ):
+                    cs = slice(j * P, (j + 1) * P)
+                    nc.tensor.matmul(
+                        out=rb[:, cs], lhsT=a_t[:, j, ts], rhs=ident_f[:], is_transpose=True, start=True, stop=False
+                    )
+                    nc.tensor.matmul(
+                        out=rb[:, cs], lhsT=b_t[:, j, ts], rhs=ident_f[:], is_transpose=True, start=False, stop=True
+                    )
+                junk = stage.tile([P, DI], BF16, tag="junk", name="junk")
+                nc.scalar.activation(out=junk[:], in_=rb[:], func=ACT.Square, accum_out=ssq[:, i : i + 1])
+            rcp = small.tile([P, 2], F32, tag="rcp", name="rcp")
+            nc.vector.reciprocal(out=rcp[:], in_=ssq[:])
+            rho = small.tile([P, 2], F32, tag="rho", name="rho")
+            nc.scalar.activation(out=rho[:], in_=rcp[:], func=ACT.Sqrt, scale=float(D))
+            ot = outs.tile([P, 2, DI], F32, tag="ot", name="ot")
+            for i in range(2):
+                nc.scalar.activation(out=ot[:, i, :], in_=rbs[i][:], func=ACT.Copy, scale=rho[:, i : i + 1])
+            nc.gpsimd.tensor_tensor(
+                out=ot[:], in0=ot[:], in1=gb[:].unsqueeze(1).to_broadcast([P, 2, DI]), op=ALU.mult
+            )
+            nc.sync.dma_start(out=o_v[h][b][:, 2 * q : 2 * q + 2, :], in_=ot[:])
+
+        prep_w(0)
+        prep_x(0)
+        prep_tab(0)
+        prep_w(1)
+        for s in range(B * NPAIR):
+            if s + 1 < B * NPAIR:
+                prep_x(s + 1)
+            if s + 1 < NPAIR:
+                prep_tab(s + 1)
+            for h in range(2):
+                group(s, h)

@@ -17,6 +17,10 @@ NT = T // P
 NPAIR = NT // 2
 NJ = DI // P
 GT = 2 * P
+NS = B * NPAIR
+NG = 2 * NS
+DUP = 4
+XE_ON_S = (1, 6, 9, 12, 15)
 FLOPS = 2 * B * T * D * 2 * DI
 
 
@@ -31,10 +35,12 @@ def tile_attentionhead_pa_t_kernel(tc, input_vecs, qk_w, sqk, cos, sin, out_0, o
     with ExitStack() as ctx:
         const = ctx.enter_context(tc.tile_pool(name="const", bufs=1))
         stage = ctx.enter_context(tc.tile_pool(name="stage", bufs=3))
-        prods = ctx.enter_context(tc.tile_pool(name="prods", bufs=3))
+        prods = ctx.enter_context(tc.tile_pool(name="prods", bufs=6))
         outs = ctx.enter_context(tc.tile_pool(name="outs", bufs=4))
         small = ctx.enter_context(tc.tile_pool(name="small", bufs=4))
-        psum = ctx.enter_context(tc.psum_pool(name="psum", bufs=4))
+        psum_mx = ctx.enter_context(tc.psum_pool(name="psum_mx", bufs=3))
+        psum_tp = ctx.enter_context(tc.psum_pool(name="psum_tp", bufs=5))
+        ctx.enter_context(tc.manual_schedule())
 
         ident_f = const.tile([P, P], F32, name="ident_f")
         make_identity(nc, ident_f[:])
@@ -43,7 +49,7 @@ def tile_attentionhead_pa_t_kernel(tc, input_vecs, qk_w, sqk, cos, sin, out_0, o
         one = const.tile([P, 1], F32, name="one")
         nc.vector.memset(one[:], 1.0)
         warm = const.tile([P, 1], F32, name="warm")
-        nc.scalar.activation(out=warm[:], in_=one[:], func=ACT.Sqrt)
+        nc.scalar.activation(out=warm[:], in_=one[:], func=ACT.Abs_reciprocal_sqrt)
 
         xr = [const.tile([P, NT, D], BF16, name="xr%d" % b) for b in range(B)]
         wr = const.tile([P, 2 * NJ, D], BF16, name="wr")
@@ -58,112 +64,177 @@ def tile_attentionhead_pa_t_kernel(tc, input_vecs, qk_w, sqk, cos, sin, out_0, o
         st = const.tile([P, NJ, NPAIR, GT], BF16, name="st")
 
         nc.sync.dma_start(out=wr[:, 0:NJ, :], in_=w_v[:, 0:NJ, :])
-        nc.sync.dma_start(out=xr[0][:, 0:2, :], in_=x_v[0][:, 0:2, :])
-        nc.sync.dma_start(out=cr[:, 0:2, :], in_=cos_v[:, 0:2, :])
-        nc.sync.dma_start(out=sr[:, 0:2, :], in_=sin_v[:, 0:2, :])
-        nc.sync.dma_start(out=wr[:, NJ : 2 * NJ, :], in_=w_v[:, NJ : 2 * NJ, :])
-        nc.sync.dma_start(out=xr[0][:, 2:NT, :], in_=x_v[0][:, 2:NT, :])
+        for lo, hi in ((0, 2), (2, 4), (4, 8)):
+            nc.sync.dma_start(out=xr[0][:, lo:hi, :], in_=x_v[0][:, lo:hi, :])
+            nc.sync.dma_start(out=cr[:, lo:hi, :], in_=cos_v[:, lo:hi, :])
+            nc.sync.dma_start(out=sr[:, lo:hi, :], in_=sin_v[:, lo:hi, :])
+            if lo == 0:
+                nc.sync.dma_start(out=wr[:, NJ : 2 * NJ, :], in_=w_v[:, NJ : 2 * NJ, :])
         nc.sync.dma_start(out=gb[:], in_=sqk.partition_broadcast(P))
-        nc.sync.dma_start(out=cr[:, 2:NT, :], in_=cos_v[:, 2:NT, :])
-        nc.sync.dma_start(out=sr[:, 2:NT, :], in_=sin_v[:, 2:NT, :])
         for b in range(1, B):
             nc.sync.dma_start(out=xr[b][:], in_=x_v[b])
 
-        def quantise_rows(rows, codes, scales, tag):
-            grouped = stage.tile([P, len(rows) * P * 4], BF16, tag=tag, name="grouped", align_bytes=64)
-            gw = grouped[:].bitcast(F32).rearrange("p (m i r u) -> p m i r u", i=2, r=P, u=2)
+        grouped = {}
+        word_banks = {}
+        banks = {}
+        prod_tiles = {}
+        r_banks = {}
+
+        def rows_tp(key, rows):
+            pts = []
             for m in range(len(rows) // 2):
-                pt = psum.tile([P, 2, 2, P], F32, tag="tp", name="pt")
+                pt = psum_tp.tile([P, 2, 2, P], F32, tag="tp", name="pt")
+                pts.append(pt)
                 for i in range(2):
                     words = rows[2 * m + i].bitcast(F32)
                     for u in range(2):
                         nc.tensor.transpose(pt[:, i, u, :], words[:, u * P : (u + 1) * P], ident_f[:])
-                nc.vector.tensor_copy(out=gw[:, m], in_=pt[:].rearrange("p i u r -> p i r u"))
-            nc.vector.quantize_mx(out=codes.bitcast(FP8X4), scales=scales, in_=grouped[:])
+            word_banks[key] = pts
 
-        def prep_w(h):
-            cols = slice(h * DI, (h + 1) * DI)
-            quantise_rows([wr[:, h * NJ + j, :] for j in range(NJ)], wc[:, cols], ws[:, cols], "wg")
-
-        def prep_x(s):
-            b, q = divmod(s, NPAIR)
-            cols = slice(s * GT, (s + 1) * GT)
-            quantise_rows([xr[b][:, 2 * q + i, :] for i in range(2)], xc[:, cols], xs[:, cols], "xg")
-
-        def prep_tab(q):
-            for raw, tab, negate in ((cr, ct, False), (sr, st, True)):
-                ptb = psum.tile([P, NJ, GT], BF16, tag="tp", name="ptb")
-                for j in range(NJ):
-                    for i in range(2):
-                        nc.tensor.transpose(
-                            ptb[:, j, i * P : (i + 1) * P], raw[:, 2 * q + i, j * P : (j + 1) * P], ident_b[:]
-                        )
-                if negate:
-                    nc.scalar.mul(out=tab[:, 0:2, q, :], in_=ptb[:, 0:2, :], mul=-1.0)
-                    nc.scalar.copy(out=tab[:, 2:4, q, :], in_=ptb[:, 2:4, :])
+        def rows_ev(key, on_scalar):
+            pts = word_banks[key]
+            g_t = stage.tile([P, len(pts) * 2 * P * 4], BF16, tag="g%d" % len(pts), name="g_t", align_bytes=64)
+            grouped[key] = g_t
+            gw = g_t[:].bitcast(F32).rearrange("p (m i r u) -> p m i r u", i=2, r=P, u=2)
+            for m in range(len(pts)):
+                src = pts[m][:].rearrange("p i u r -> p i r u")
+                if on_scalar:
+                    nc.scalar.copy(out=gw[:, m], in_=src)
                 else:
-                    nc.scalar.copy(out=tab[:, :, q, :], in_=ptb[:])
+                    nc.vector.tensor_copy(out=gw[:, m], in_=src)
 
-        def group(s, h):
+        def w_t(h, on_scalar):
+            rows_tp(("w", h), [wr[:, h * NJ + j, :] for j in range(NJ)])
+            rows_ev(("w", h), on_scalar)
+
+        def w_q(h):
+            cols = slice(h * DI, (h + 1) * DI)
+            nc.vector.quantize_mx(out=wc[:, cols].bitcast(FP8X4), scales=ws[:, cols], in_=grouped[("w", h)][:])
+
+        def x_tp(s):
             b, q = divmod(s, NPAIR)
+            rows_tp(("x", s), [xr[b][:, 2 * q + i, :] for i in range(2)])
+
+        def x_q(s):
+            cols = slice(s * GT, (s + 1) * GT)
+            nc.vector.quantize_mx(out=xc[:, cols].bitcast(FP8X4), scales=xs[:, cols], in_=grouped[("x", s)][:])
+
+        def tab(q, is_sin):
+            raw = sr if is_sin else cr
+            ptb = psum_tp.tile([P, NJ, GT], BF16, tag="tp", name="ptb")
+            for j in range(NJ):
+                for i in range(2):
+                    nc.tensor.transpose(
+                        ptb[:, j, i * P : (i + 1) * P], raw[:, 2 * q + i, j * P : (j + 1) * P], ident_b[:]
+                    )
+            if is_sin:
+                nc.scalar.copy(out=st[:, 0:2, q, :], in_=ptb[:, 2:4, :])
+                nc.scalar.mul(out=st[:, 2:4, q, :], in_=ptb[:, 0:2, :], mul=-1.0)
+            else:
+                nc.scalar.copy(out=ct[:, :, q, :], in_=ptb[:])
+
+        def mx(g):
+            s, h = divmod(g, 2)
             tok = slice(s * GT, (s + 1) * GT)
-            banks = []
-            for half in range(2):
-                u = psum.tile([P, 2, GT], F32, tag="mx", name="u")
-                banks.append(u)
-                for jj in range(2):
-                    c0 = h * DI + (2 * half + jj) * P
-                    nc.tensor.matmul_mx(
-                        out=u[:, jj, :],
-                        lhsT=wc[:, c0 : c0 + P].bitcast(FP8X4),
-                        lhsT_scale=ws[:, c0 : c0 + P],
-                        rhs=xc[:, tok].bitcast(FP8X4),
-                        rhs_scale=xs[:, tok],
-                        start=True,
-                        stop=True,
-                    )
-            a_t = prods.tile([P, NJ, GT], F32, tag="a", name="a_t")
-            b_t = prods.tile([P, NJ, GT], F32, tag="b", name="b_t")
-            for half in range(2):
-                js = slice(2 * half, 2 * half + 2)
-                nc.vector.tensor_tensor(out=a_t[:, js, :], in0=banks[half][:], in1=ct[:, js, q, :], op=ALU.mult)
-                nc.vector.tensor_tensor(out=b_t[:, js, :], in0=banks[1 - half][:], in1=st[:, js, q, :], op=ALU.mult)
-            ssq = small.tile([P, 2], F32, tag="ssq", name="ssq")
-            rbs = []
+            banks[g] = []
+            for pr in range(2):
+                x2 = psum_mx.tile([P, 2, GT], F32, tag="mx", name="x2")
+                banks[g].append(x2)
+                for t2 in range(2):
+                    c0 = h * DI + (pr + 2 * t2) * P
+                    for rep in range(2 if 2 * pr + t2 < DUP else 1):
+                        nc.tensor.matmul_mx(
+                            out=x2[:, t2, :],
+                            lhsT=wc[:, c0 : c0 + P].bitcast(FP8X4),
+                            lhsT_scale=ws[:, c0 : c0 + P],
+                            rhs=xc[:, tok].bitcast(FP8X4),
+                            rhs_scale=xs[:, tok],
+                            start=True,
+                            stop=True,
+                        )
+
+        def prod(g, pr):
+            q = (g // 2) % NPAIR
+            js = slice(pr, NJ, 2)
+            a2 = prods.tile([P, 2, GT], F32, tag="a", name="a2")
+            b2 = prods.tile([P, 2, GT], F32, tag="b", name="b2")
+            prod_tiles[(g, pr)] = (a2, b2)
+            nc.vector.tensor_tensor(out=a2[:], in0=banks[g][pr][:], in1=ct[:, js, q, :], op=ALU.mult)
+            nc.vector.tensor_tensor(out=b2[:], in0=banks[g][pr][:], in1=st[:, js, q, :], op=ALU.mult)
+
+        def add_t(g):
+            r_banks[g] = []
             for i in range(2):
-                rb = psum.tile([P, DI], F32, tag="tp", name="rb")
-                rbs.append(rb)
+                rb = psum_tp.tile([P, DI], F32, tag="tp", name="rb")
+                r_banks[g].append(rb)
                 ts = slice(i * P, (i + 1) * P)
-                for j in range(NJ):
-                    cs = slice(j * P, (j + 1) * P)
-                    nc.tensor.matmul(
-                        out=rb[:, cs], lhsT=a_t[:, j, ts], rhs=ident_f[:], is_transpose=True, start=True, stop=False
-                    )
-                    nc.tensor.matmul(
-                        out=rb[:, cs], lhsT=b_t[:, j, ts], rhs=ident_f[:], is_transpose=True, start=False, stop=True
-                    )
+                for pr in range(2):
+                    a2, b2 = prod_tiles[(g, pr)]
+                    for t2 in range(2):
+                        j = pr + 2 * t2
+                        cs = slice(j * P, (j + 1) * P)
+                        nc.tensor.matmul(
+                            out=rb[:, cs], lhsT=a2[:, t2, ts], rhs=ident_f[:], is_transpose=True, start=True, stop=False
+                        )
+                        nc.tensor.matmul(
+                            out=rb[:, cs],
+                            lhsT=b2[:, 1 - t2, ts],
+                            rhs=ident_f[:],
+                            is_transpose=True,
+                            start=False,
+                            stop=True,
+                        )
+
+        def finish(g):
+            s, h = divmod(g, 2)
+            b, q = divmod(s, NPAIR)
+            ssq = small.tile([P, 2], F32, tag="ssq", name="ssq")
+            for i in range(2):
                 junk = stage.tile([P, DI], BF16, tag="junk", name="junk")
-                nc.scalar.activation(out=junk[:], in_=rb[:], func=ACT.Square, accum_out=ssq[:, i : i + 1])
-            rcp = small.tile([P, 2], F32, tag="rcp", name="rcp")
-            nc.vector.reciprocal(out=rcp[:], in_=ssq[:])
+                nc.scalar.activation(out=junk[:], in_=r_banks[g][i][:], func=ACT.Square, accum_out=ssq[:, i : i + 1])
             rho = small.tile([P, 2], F32, tag="rho", name="rho")
-            nc.scalar.activation(out=rho[:], in_=rcp[:], func=ACT.Sqrt, scale=float(D))
+            nc.scalar.activation(out=rho[:], in_=ssq[:], func=ACT.Abs_reciprocal_sqrt, scale=1.0 / D)
             ot = outs.tile([P, 2, DI], F32, tag="ot", name="ot")
             for i in range(2):
-                nc.scalar.activation(out=ot[:, i, :], in_=rbs[i][:], func=ACT.Copy, scale=rho[:, i : i + 1])
+                nc.scalar.activation(out=ot[:, i, :], in_=r_banks[g][i][:], func=ACT.Copy, scale=rho[:, i : i + 1])
             nc.gpsimd.tensor_tensor(
                 out=ot[:], in0=ot[:], in1=gb[:].unsqueeze(1).to_broadcast([P, 2, DI]), op=ALU.mult
             )
             nc.sync.dma_start(out=o_v[h][b][:, 2 * q : 2 * q + 2, :], in_=ot[:])
 
-        prep_w(0)
-        prep_x(0)
-        prep_tab(0)
-        prep_w(1)
-        for s in range(B * NPAIR):
-            if s + 1 < B * NPAIR:
-                prep_x(s + 1)
-            if s + 1 < NPAIR:
-                prep_tab(s + 1)
-            for h in range(2):
-                group(s, h)
+        w_t(0, False)
+        x_tp(0)
+        rows_ev(("x", 0), False)
+        w_q(0)
+        x_q(0)
+        tab(0, False)
+        tab(0, True)
+        mx(0)
+        w_t(1, True)
+        x_tp(1)
+        rows_ev(("x", 1), True)
+
+        tab_at = {0: ((1, False), (1, True)), 1: ((2, False),), 2: ((2, True),), 3: ((3, False),), 4: ((3, True),)}
+        for it in range(NG + 1):
+            s_new = (it + 3) // 2 if it % 2 == 1 and (it + 3) // 2 < NS else None
+            if it >= 1:
+                add_t(it - 1)
+            if s_new is not None:
+                x_tp(s_new)
+            if it < NG:
+                prod(it, 0)
+                if it == 0:
+                    w_q(1)
+                prod(it, 1)
+            if s_new is not None and s_new not in XE_ON_S:
+                rows_ev(("x", s_new), False)
+            if it % 2 == 0 and (it + 2) // 2 < NS:
+                x_q((it + 2) // 2)
+            if it + 1 < NG:
+                mx(it + 1)
+            if it >= 1:
+                finish(it - 1)
+            if s_new is not None and s_new in XE_ON_S:
+                rows_ev(("x", s_new), True)
+            for q, is_sin in tab_at.get(it, ()):
+                tab(q, is_sin)

@@ -38,8 +38,8 @@ def tile_attentionhead_pa_t_kernel(tc, input_vecs, qk_w, sqk, cos, sin, out_0, o
         prods = ctx.enter_context(tc.tile_pool(name="prods", bufs=6))
         outs = ctx.enter_context(tc.tile_pool(name="outs", bufs=4))
         small = ctx.enter_context(tc.tile_pool(name="small", bufs=4))
-        psum_mx = ctx.enter_context(tc.psum_pool(name="psum_mx", bufs=3))
-        psum_tp = ctx.enter_context(tc.psum_pool(name="psum_tp", bufs=5))
+        psum_mx = ctx.enter_context(tc.psum_pool(name="psum_mx", bufs=4))
+        psum_tp = ctx.enter_context(tc.psum_pool(name="psum_tp", bufs=4))
         ctx.enter_context(tc.manual_schedule())
 
         ident_f = const.tile([P, P], F32, name="ident_f")
@@ -195,6 +195,18 @@ def tile_attentionhead_pa_t_kernel(tc, input_vecs, qk_w, sqk, cos, sin, out_0, o
             rho = small.tile([P, 2], F32, tag="rho", name="rho")
             nc.scalar.activation(out=rho[:], in_=ssq[:], func=ACT.Abs_reciprocal_sqrt, scale=1.0 / D)
             ot = outs.tile([P, 2, DI], F32, tag="ot", name="ot")
+            if g == NG - 1:
+                for i in range(2):
+                    nc.vector.scalar_tensor_tensor(
+                        out=ot[:, i, :],
+                        in0=r_banks[g][i][:],
+                        scalar=rho[:, i : i + 1],
+                        in1=gb[:],
+                        op0=ALU.mult,
+                        op1=ALU.mult,
+                    )
+                    nc.sync.dma_start(out=o_v[h][b][:, 2 * q + i, :], in_=ot[:, i, :])
+                return
             for i in range(2):
                 nc.scalar.activation(out=ot[:, i, :], in_=r_banks[g][i][:], func=ACT.Copy, scale=rho[:, i : i + 1])
             nc.gpsimd.tensor_tensor(
@@ -216,22 +228,26 @@ def tile_attentionhead_pa_t_kernel(tc, input_vecs, qk_w, sqk, cos, sin, out_0, o
 
         tab_at = {0: ((1, False), (1, True)), 1: ((2, False),), 2: ((2, True),), 3: ((3, False),), 4: ((3, True),)}
         for it in range(NG + 1):
-            s_new = (it + 3) // 2 if it % 2 == 1 and (it + 3) // 2 < NS else None
+            s_new = (it + 4) // 2 if it % 2 == 0 and (it + 4) // 2 < NS else None
             if it >= 1:
+                if it + 1 < NG:
+                    mx(it + 1)
                 add_t(it - 1)
-            if s_new is not None:
-                x_tp(s_new)
+                if s_new is not None:
+                    x_tp(s_new)
             if it < NG:
                 prod(it, 0)
                 if it == 0:
                     w_q(1)
                 prod(it, 1)
+            if it == 0:
+                x_q(1)
+                mx(1)
+                x_tp(s_new)
+            if it % 2 == 1 and (it + 3) // 2 < NS:
+                x_q((it + 3) // 2)
             if s_new is not None and s_new not in XE_ON_S:
                 rows_ev(("x", s_new), False)
-            if it % 2 == 0 and (it + 2) // 2 < NS:
-                x_q((it + 2) // 2)
-            if it + 1 < NG:
-                mx(it + 1)
             if it >= 1:
                 finish(it - 1)
             if s_new is not None and s_new in XE_ON_S:

@@ -19,8 +19,8 @@ NJ = DI // P
 GT = 2 * P
 NS = B * NPAIR
 NG = 2 * NS
-DUP = 4
-XE_ON_S = (1, 6, 9, 12, 15)
+DUP = 3
+XE_ON_S = (1, 9, 13)
 FLOPS = 2 * B * T * D * 2 * DI
 
 
@@ -38,8 +38,8 @@ def tile_attentionhead_pa_t_kernel(tc, input_vecs, qk_w, sqk, cos, sin, out_0, o
         prods = ctx.enter_context(tc.tile_pool(name="prods", bufs=6))
         outs = ctx.enter_context(tc.tile_pool(name="outs", bufs=4))
         small = ctx.enter_context(tc.tile_pool(name="small", bufs=4))
-        psum_mx = ctx.enter_context(tc.psum_pool(name="psum_mx", bufs=4))
-        psum_tp = ctx.enter_context(tc.psum_pool(name="psum_tp", bufs=4))
+        psum_mx = ctx.enter_context(tc.psum_pool(name="psum_mx", bufs=3))
+        psum_tp = ctx.enter_context(tc.psum_pool(name="psum_tp", bufs=5))
         ctx.enter_context(tc.manual_schedule())
 
         ident_f = const.tile([P, P], F32, name="ident_f")
@@ -60,16 +60,16 @@ def tile_attentionhead_pa_t_kernel(tc, input_vecs, qk_w, sqk, cos, sin, out_0, o
         xs = const.tile([P, B * T], U8, name="xs", align_bytes=64)
         wc = const.tile([P, 2 * DI], U32, name="wc", align_bytes=64)
         ws = const.tile([P, 2 * DI], U8, name="ws", align_bytes=64)
-        ct = const.tile([P, NJ, NPAIR, GT], BF16, name="ct")
-        st = const.tile([P, NJ, NPAIR, GT], BF16, name="st")
+        tabs = const.tile([P, 2, NJ, NPAIR, GT], BF16, name="tabs")
 
         nc.sync.dma_start(out=wr[:, 0:NJ, :], in_=w_v[:, 0:NJ, :])
+        nc.sync.dma_start(out=xr[0][:, 0:2, :], in_=x_v[0][:, 0:2, :])
+        nc.sync.dma_start(out=wr[:, NJ : 2 * NJ, :], in_=w_v[:, NJ : 2 * NJ, :])
         for lo, hi in ((0, 2), (2, 4), (4, 8)):
-            nc.sync.dma_start(out=xr[0][:, lo:hi, :], in_=x_v[0][:, lo:hi, :])
+            if lo > 0:
+                nc.sync.dma_start(out=xr[0][:, lo:hi, :], in_=x_v[0][:, lo:hi, :])
             nc.sync.dma_start(out=cr[:, lo:hi, :], in_=cos_v[:, lo:hi, :])
             nc.sync.dma_start(out=sr[:, lo:hi, :], in_=sin_v[:, lo:hi, :])
-            if lo == 0:
-                nc.sync.dma_start(out=wr[:, NJ : 2 * NJ, :], in_=w_v[:, NJ : 2 * NJ, :])
         nc.sync.dma_start(out=gb[:], in_=sqk.partition_broadcast(P))
         for b in range(1, B):
             nc.sync.dma_start(out=xr[b][:], in_=x_v[b])
@@ -98,14 +98,13 @@ def tile_attentionhead_pa_t_kernel(tc, input_vecs, qk_w, sqk, cos, sin, out_0, o
             gw = g_t[:].bitcast(F32).rearrange("p (m i r u) -> p m i r u", i=2, r=P, u=2)
             for m in range(len(pts)):
                 src = pts[m][:].rearrange("p i u r -> p i r u")
-                if on_scalar:
+                if on_scalar[m]:
                     nc.scalar.copy(out=gw[:, m], in_=src)
                 else:
                     nc.vector.tensor_copy(out=gw[:, m], in_=src)
 
-        def w_t(h, on_scalar):
+        def w_tp(h):
             rows_tp(("w", h), [wr[:, h * NJ + j, :] for j in range(NJ)])
-            rows_ev(("w", h), on_scalar)
 
         def w_q(h):
             cols = slice(h * DI, (h + 1) * DI)
@@ -128,12 +127,12 @@ def tile_attentionhead_pa_t_kernel(tc, input_vecs, qk_w, sqk, cos, sin, out_0, o
                         ptb[:, j, i * P : (i + 1) * P], raw[:, 2 * q + i, j * P : (j + 1) * P], ident_b[:]
                     )
             if is_sin:
-                nc.scalar.copy(out=st[:, 0:2, q, :], in_=ptb[:, 2:4, :])
-                nc.scalar.mul(out=st[:, 2:4, q, :], in_=ptb[:, 0:2, :], mul=-1.0)
+                nc.scalar.copy(out=tabs[:, 1, 0:2, q, :], in_=ptb[:, 2:4, :])
+                nc.scalar.mul(out=tabs[:, 1, 2:4, q, :], in_=ptb[:, 0:2, :], mul=-1.0)
             else:
-                nc.scalar.copy(out=ct[:, :, q, :], in_=ptb[:])
+                nc.scalar.copy(out=tabs[:, 0, :, q, :], in_=ptb[:])
 
-        def mx(g):
+        def mx(g, dup):
             s, h = divmod(g, 2)
             tok = slice(s * GT, (s + 1) * GT)
             banks[g] = []
@@ -142,7 +141,7 @@ def tile_attentionhead_pa_t_kernel(tc, input_vecs, qk_w, sqk, cos, sin, out_0, o
                 banks[g].append(x2)
                 for t2 in range(2):
                     c0 = h * DI + (pr + 2 * t2) * P
-                    for rep in range(2 if 2 * pr + t2 < DUP else 1):
+                    for rep in range(2 if 2 * pr + t2 < dup else 1):
                         nc.tensor.matmul_mx(
                             out=x2[:, t2, :],
                             lhsT=wc[:, c0 : c0 + P].bitcast(FP8X4),
@@ -155,12 +154,14 @@ def tile_attentionhead_pa_t_kernel(tc, input_vecs, qk_w, sqk, cos, sin, out_0, o
 
         def prod(g, pr):
             q = (g // 2) % NPAIR
-            js = slice(pr, NJ, 2)
-            a2 = prods.tile([P, 2, GT], F32, tag="a", name="a2")
-            b2 = prods.tile([P, 2, GT], F32, tag="b", name="b2")
-            prod_tiles[(g, pr)] = (a2, b2)
-            nc.vector.tensor_tensor(out=a2[:], in0=banks[g][pr][:], in1=ct[:, js, q, :], op=ALU.mult)
-            nc.vector.tensor_tensor(out=b2[:], in0=banks[g][pr][:], in1=st[:, js, q, :], op=ALU.mult)
+            ab = prods.tile([P, 2, 2, GT], F32, tag="ab", name="ab")
+            prod_tiles[(g, pr)] = ab
+            nc.vector.tensor_tensor(
+                out=ab[:],
+                in0=banks[g][pr][:].unsqueeze(1).to_broadcast([P, 2, 2, GT]),
+                in1=tabs[:, :, slice(pr, NJ, 2), q, :],
+                op=ALU.mult,
+            )
 
         def add_t(g):
             r_banks[g] = []
@@ -169,38 +170,46 @@ def tile_attentionhead_pa_t_kernel(tc, input_vecs, qk_w, sqk, cos, sin, out_0, o
                 r_banks[g].append(rb)
                 ts = slice(i * P, (i + 1) * P)
                 for pr in range(2):
-                    a2, b2 = prod_tiles[(g, pr)]
+                    ab = prod_tiles[(g, pr)]
                     for t2 in range(2):
                         j = pr + 2 * t2
                         cs = slice(j * P, (j + 1) * P)
                         nc.tensor.matmul(
-                            out=rb[:, cs], lhsT=a2[:, t2, ts], rhs=ident_f[:], is_transpose=True, start=True, stop=False
+                            out=rb[:, cs],
+                            lhsT=ab[:, 0, t2, ts],
+                            rhs=ident_f[:],
+                            is_transpose=True,
+                            start=True,
+                            stop=False,
                         )
                         nc.tensor.matmul(
                             out=rb[:, cs],
-                            lhsT=b2[:, 1 - t2, ts],
+                            lhsT=ab[:, 1, 1 - t2, ts],
                             rhs=ident_f[:],
                             is_transpose=True,
                             start=False,
                             stop=True,
                         )
 
+        def sum_squares(g, i, ssq):
+            junk = stage.tile([P, DI], BF16, tag="junk", name="junk")
+            nc.scalar.activation(out=junk[:], in_=r_banks[g][i][:], func=ACT.Square, accum_out=ssq[:, i : i + 1])
+
         def finish(g):
             s, h = divmod(g, 2)
             b, q = divmod(s, NPAIR)
             ssq = small.tile([P, 2], F32, tag="ssq", name="ssq")
-            for i in range(2):
-                junk = stage.tile([P, DI], BF16, tag="junk", name="junk")
-                nc.scalar.activation(out=junk[:], in_=r_banks[g][i][:], func=ACT.Square, accum_out=ssq[:, i : i + 1])
             rho = small.tile([P, 2], F32, tag="rho", name="rho")
-            nc.scalar.activation(out=rho[:], in_=ssq[:], func=ACT.Abs_reciprocal_sqrt, scale=1.0 / D)
             ot = outs.tile([P, 2, DI], F32, tag="ot", name="ot")
             if g == NG - 1:
                 for i in range(2):
+                    col = slice(i, i + 1)
+                    sum_squares(g, i, ssq)
+                    nc.scalar.activation(out=rho[:, col], in_=ssq[:, col], func=ACT.Abs_reciprocal_sqrt, scale=1.0 / D)
                     nc.vector.scalar_tensor_tensor(
                         out=ot[:, i, :],
                         in0=r_banks[g][i][:],
-                        scalar=rho[:, i : i + 1],
+                        scalar=rho[:, col],
                         in1=gb[:],
                         op0=ALU.mult,
                         op1=ALU.mult,
@@ -208,49 +217,49 @@ def tile_attentionhead_pa_t_kernel(tc, input_vecs, qk_w, sqk, cos, sin, out_0, o
                     nc.sync.dma_start(out=o_v[h][b][:, 2 * q + i, :], in_=ot[:, i, :])
                 return
             for i in range(2):
+                sum_squares(g, i, ssq)
+            nc.scalar.activation(out=rho[:], in_=ssq[:], func=ACT.Abs_reciprocal_sqrt, scale=1.0 / D)
+            for i in range(2):
                 nc.scalar.activation(out=ot[:, i, :], in_=r_banks[g][i][:], func=ACT.Copy, scale=rho[:, i : i + 1])
             nc.gpsimd.tensor_tensor(
                 out=ot[:], in0=ot[:], in1=gb[:].unsqueeze(1).to_broadcast([P, 2, DI]), op=ALU.mult
             )
             nc.sync.dma_start(out=o_v[h][b][:, 2 * q : 2 * q + 2, :], in_=ot[:])
 
-        w_t(0, False)
+        w_tp(0)
+        rows_ev(("w", 0), (False, True))
         x_tp(0)
-        rows_ev(("x", 0), False)
+        rows_ev(("x", 0), (False,))
         w_q(0)
         x_q(0)
+        w_tp(1)
+        rows_ev(("w", 1), (True, False))
+        w_q(1)
         tab(0, False)
         tab(0, True)
-        mx(0)
-        w_t(1, True)
+        mx(0, 0)
         x_tp(1)
-        rows_ev(("x", 1), True)
+        rows_ev(("x", 1), (True,))
 
         tab_at = {0: ((1, False), (1, True)), 1: ((2, False),), 2: ((2, True),), 3: ((3, False),), 4: ((3, True),)}
         for it in range(NG + 1):
-            s_new = (it + 4) // 2 if it % 2 == 0 and (it + 4) // 2 < NS else None
+            s_new = (it + 3) // 2 if it % 2 == 1 and (it + 3) // 2 < NS else None
             if it >= 1:
-                if it + 1 < NG:
-                    mx(it + 1)
                 add_t(it - 1)
-                if s_new is not None:
-                    x_tp(s_new)
+            if s_new is not None:
+                x_tp(s_new)
             if it < NG:
                 prod(it, 0)
-                if it == 0:
-                    w_q(1)
                 prod(it, 1)
-            if it == 0:
-                x_q(1)
-                mx(1)
-                x_tp(s_new)
-            if it % 2 == 1 and (it + 3) // 2 < NS:
-                x_q((it + 3) // 2)
             if s_new is not None and s_new not in XE_ON_S:
-                rows_ev(("x", s_new), False)
+                rows_ev(("x", s_new), (False,))
+            if it % 2 == 0 and (it + 2) // 2 < NS:
+                x_q((it + 2) // 2)
+            if it + 1 < NG:
+                mx(it + 1, DUP)
             if it >= 1:
                 finish(it - 1)
             if s_new is not None and s_new in XE_ON_S:
-                rows_ev(("x", s_new), True)
+                rows_ev(("x", s_new), (True,))
             for q, is_sin in tab_at.get(it, ()):
                 tab(q, is_sin)

@@ -19,7 +19,7 @@ NJ = DI // P
 GT = 2 * P
 NS = B * NPAIR
 NG = 2 * NS
-DUP = 3
+REPS = 2
 XE_ON_S = (1, 9, 13)
 FLOPS = 2 * B * T * D * 2 * DI
 
@@ -132,25 +132,23 @@ def tile_attentionhead_pa_t_kernel(tc, input_vecs, qk_w, sqk, cos, sin, out_0, o
             else:
                 nc.scalar.copy(out=tabs[:, 0, :, q, :], in_=ptb[:])
 
-        def mx(g, dup):
+        def mx_half(g, pr, reps):
             s, h = divmod(g, 2)
             tok = slice(s * GT, (s + 1) * GT)
-            banks[g] = []
-            for pr in range(2):
-                x2 = psum_mx.tile([P, 2, GT], F32, tag="mx", name="x2")
-                banks[g].append(x2)
-                for t2 in range(2):
-                    c0 = h * DI + (pr + 2 * t2) * P
-                    for rep in range(2 if 2 * pr + t2 < dup else 1):
-                        nc.tensor.matmul_mx(
-                            out=x2[:, t2, :],
-                            lhsT=wc[:, c0 : c0 + P].bitcast(FP8X4),
-                            lhsT_scale=ws[:, c0 : c0 + P],
-                            rhs=xc[:, tok].bitcast(FP8X4),
-                            rhs_scale=xs[:, tok],
-                            start=True,
-                            stop=True,
-                        )
+            x2 = psum_mx.tile([P, 2, GT], F32, tag="mx", name="x2")
+            banks[(g, pr)] = x2
+            for t2 in range(2):
+                c0 = h * DI + (pr + 2 * t2) * P
+                for rep in range(reps):
+                    nc.tensor.matmul_mx(
+                        out=x2[:, t2, :],
+                        lhsT=wc[:, c0 : c0 + P].bitcast(FP8X4),
+                        lhsT_scale=ws[:, c0 : c0 + P],
+                        rhs=xc[:, tok].bitcast(FP8X4),
+                        rhs_scale=xs[:, tok],
+                        start=True,
+                        stop=True,
+                    )
 
         def prod(g, pr):
             q = (g // 2) % NPAIR
@@ -158,16 +156,15 @@ def tile_attentionhead_pa_t_kernel(tc, input_vecs, qk_w, sqk, cos, sin, out_0, o
             prod_tiles[(g, pr)] = ab
             nc.vector.tensor_tensor(
                 out=ab[:],
-                in0=banks[g][pr][:].unsqueeze(1).to_broadcast([P, 2, 2, GT]),
+                in0=banks[(g, pr)][:].unsqueeze(1).to_broadcast([P, 2, 2, GT]),
                 in1=tabs[:, :, slice(pr, NJ, 2), q, :],
                 op=ALU.mult,
             )
 
-        def add_t(g):
-            r_banks[g] = []
-            for i in range(2):
+        def add_t(g, i):
+            if True:
                 rb = psum_tp.tile([P, DI], F32, tag="tp", name="rb")
-                r_banks[g].append(rb)
+                r_banks[(g, i)] = rb
                 ts = slice(i * P, (i + 1) * P)
                 for pr in range(2):
                     ab = prod_tiles[(g, pr)]
@@ -193,7 +190,7 @@ def tile_attentionhead_pa_t_kernel(tc, input_vecs, qk_w, sqk, cos, sin, out_0, o
 
         def sum_squares(g, i, ssq):
             junk = stage.tile([P, DI], BF16, tag="junk", name="junk")
-            nc.scalar.activation(out=junk[:], in_=r_banks[g][i][:], func=ACT.Square, accum_out=ssq[:, i : i + 1])
+            nc.scalar.activation(out=junk[:], in_=r_banks[(g, i)][:], func=ACT.Square, accum_out=ssq[:, i : i + 1])
 
         def finish(g):
             s, h = divmod(g, 2)
@@ -208,7 +205,7 @@ def tile_attentionhead_pa_t_kernel(tc, input_vecs, qk_w, sqk, cos, sin, out_0, o
                     nc.scalar.activation(out=rho[:, col], in_=ssq[:, col], func=ACT.Abs_reciprocal_sqrt, scale=1.0 / D)
                     nc.vector.scalar_tensor_tensor(
                         out=ot[:, i, :],
-                        in0=r_banks[g][i][:],
+                        in0=r_banks[(g, i)][:],
                         scalar=rho[:, col],
                         in1=gb[:],
                         op0=ALU.mult,
@@ -220,7 +217,7 @@ def tile_attentionhead_pa_t_kernel(tc, input_vecs, qk_w, sqk, cos, sin, out_0, o
                 sum_squares(g, i, ssq)
             nc.scalar.activation(out=rho[:], in_=ssq[:], func=ACT.Abs_reciprocal_sqrt, scale=1.0 / D)
             for i in range(2):
-                nc.scalar.activation(out=ot[:, i, :], in_=r_banks[g][i][:], func=ACT.Copy, scale=rho[:, i : i + 1])
+                nc.scalar.activation(out=ot[:, i, :], in_=r_banks[(g, i)][:], func=ACT.Copy, scale=rho[:, i : i + 1])
             nc.gpsimd.tensor_tensor(
                 out=ot[:], in0=ot[:], in1=gb[:].unsqueeze(1).to_broadcast([P, 2, DI]), op=ALU.mult
             )
@@ -237,7 +234,8 @@ def tile_attentionhead_pa_t_kernel(tc, input_vecs, qk_w, sqk, cos, sin, out_0, o
         w_q(1)
         tab(0, False)
         tab(0, True)
-        mx(0, 0)
+        mx_half(0, 0, 1)
+        mx_half(0, 1, 1)
         x_tp(1)
         rows_ev(("x", 1), (True,))
 
@@ -245,7 +243,11 @@ def tile_attentionhead_pa_t_kernel(tc, input_vecs, qk_w, sqk, cos, sin, out_0, o
         for it in range(NG + 1):
             s_new = (it + 3) // 2 if it % 2 == 1 and (it + 3) // 2 < NS else None
             if it >= 1:
-                add_t(it - 1)
+                add_t(it - 1, 0)
+            if it + 1 < NG:
+                mx_half(it + 1, 0, REPS)
+            if it >= 1:
+                add_t(it - 1, 1)
             if s_new is not None:
                 x_tp(s_new)
             if it < NG:
@@ -256,7 +258,7 @@ def tile_attentionhead_pa_t_kernel(tc, input_vecs, qk_w, sqk, cos, sin, out_0, o
             if it % 2 == 0 and (it + 2) // 2 < NS:
                 x_q((it + 2) // 2)
             if it + 1 < NG:
-                mx(it + 1, DUP)
+                mx_half(it + 1, 1, REPS)
             if it >= 1:
                 finish(it - 1)
             if s_new is not None and s_new in XE_ON_S:

@@ -19,7 +19,7 @@ NJ = DI // P
 GT = 2 * P
 NS = B * NPAIR
 NG = 2 * NS
-REPS = 2
+DUP = 0
 XE_ON_S = (1, 9, 13)
 FLOPS = 2 * B * T * D * 2 * DI
 
@@ -132,23 +132,25 @@ def tile_attentionhead_pa_t_kernel(tc, input_vecs, qk_w, sqk, cos, sin, out_0, o
             else:
                 nc.scalar.copy(out=tabs[:, 0, :, q, :], in_=ptb[:])
 
-        def mx_half(g, pr, reps):
+        def mx(g, dup):
             s, h = divmod(g, 2)
             tok = slice(s * GT, (s + 1) * GT)
-            x2 = psum_mx.tile([P, 2, GT], F32, tag="mx", name="x2")
-            banks[(g, pr)] = x2
-            for t2 in range(2):
-                c0 = h * DI + (pr + 2 * t2) * P
-                for rep in range(reps):
-                    nc.tensor.matmul_mx(
-                        out=x2[:, t2, :],
-                        lhsT=wc[:, c0 : c0 + P].bitcast(FP8X4),
-                        lhsT_scale=ws[:, c0 : c0 + P],
-                        rhs=xc[:, tok].bitcast(FP8X4),
-                        rhs_scale=xs[:, tok],
-                        start=True,
-                        stop=True,
-                    )
+            banks[g] = []
+            for pr in range(2):
+                x2 = psum_mx.tile([P, 2, GT], F32, tag="mx", name="x2")
+                banks[g].append(x2)
+                for t2 in range(2):
+                    c0 = h * DI + (pr + 2 * t2) * P
+                    for rep in range(2 if 2 * pr + t2 < dup else 1):
+                        nc.tensor.matmul_mx(
+                            out=x2[:, t2, :],
+                            lhsT=wc[:, c0 : c0 + P].bitcast(FP8X4),
+                            lhsT_scale=ws[:, c0 : c0 + P],
+                            rhs=xc[:, tok].bitcast(FP8X4),
+                            rhs_scale=xs[:, tok],
+                            start=True,
+                            stop=True,
+                        )
 
         def prod(g, pr):
             q = (g // 2) % NPAIR
@@ -156,15 +158,16 @@ def tile_attentionhead_pa_t_kernel(tc, input_vecs, qk_w, sqk, cos, sin, out_0, o
             prod_tiles[(g, pr)] = ab
             nc.vector.tensor_tensor(
                 out=ab[:],
-                in0=banks[(g, pr)][:].unsqueeze(1).to_broadcast([P, 2, 2, GT]),
+                in0=banks[g][pr][:].unsqueeze(1).to_broadcast([P, 2, 2, GT]),
                 in1=tabs[:, :, slice(pr, NJ, 2), q, :],
                 op=ALU.mult,
             )
 
-        def add_t(g, i):
-            if True:
+        def add_t(g):
+            r_banks[g] = []
+            for i in range(2):
                 rb = psum_tp.tile([P, DI], F32, tag="tp", name="rb")
-                r_banks[(g, i)] = rb
+                r_banks[g].append(rb)
                 ts = slice(i * P, (i + 1) * P)
                 for pr in range(2):
                     ab = prod_tiles[(g, pr)]
@@ -190,7 +193,7 @@ def tile_attentionhead_pa_t_kernel(tc, input_vecs, qk_w, sqk, cos, sin, out_0, o
 
         def sum_squares(g, i, ssq):
             junk = stage.tile([P, DI], BF16, tag="junk", name="junk")
-            nc.scalar.activation(out=junk[:], in_=r_banks[(g, i)][:], func=ACT.Square, accum_out=ssq[:, i : i + 1])
+            nc.scalar.activation(out=junk[:], in_=r_banks[g][i][:], func=ACT.Square, accum_out=ssq[:, i : i + 1])
 
         def finish(g):
             s, h = divmod(g, 2)
@@ -205,7 +208,7 @@ def tile_attentionhead_pa_t_kernel(tc, input_vecs, qk_w, sqk, cos, sin, out_0, o
                     nc.scalar.activation(out=rho[:, col], in_=ssq[:, col], func=ACT.Abs_reciprocal_sqrt, scale=1.0 / D)
                     nc.vector.scalar_tensor_tensor(
                         out=ot[:, i, :],
-                        in0=r_banks[(g, i)][:],
+                        in0=r_banks[g][i][:],
                         scalar=rho[:, col],
                         in1=gb[:],
                         op0=ALU.mult,
@@ -217,7 +220,7 @@ def tile_attentionhead_pa_t_kernel(tc, input_vecs, qk_w, sqk, cos, sin, out_0, o
                 sum_squares(g, i, ssq)
             nc.scalar.activation(out=rho[:], in_=ssq[:], func=ACT.Abs_reciprocal_sqrt, scale=1.0 / D)
             for i in range(2):
-                nc.scalar.activation(out=ot[:, i, :], in_=r_banks[(g, i)][:], func=ACT.Copy, scale=rho[:, i : i + 1])
+                nc.scalar.activation(out=ot[:, i, :], in_=r_banks[g][i][:], func=ACT.Copy, scale=rho[:, i : i + 1])
             nc.gpsimd.tensor_tensor(
                 out=ot[:], in0=ot[:], in1=gb[:].unsqueeze(1).to_broadcast([P, 2, DI]), op=ALU.mult
             )
@@ -234,8 +237,7 @@ def tile_attentionhead_pa_t_kernel(tc, input_vecs, qk_w, sqk, cos, sin, out_0, o
         w_q(1)
         tab(0, False)
         tab(0, True)
-        mx_half(0, 0, 1)
-        mx_half(0, 1, 1)
+        mx(0, 0)
         x_tp(1)
         rows_ev(("x", 1), (True,))
 
@@ -243,11 +245,7 @@ def tile_attentionhead_pa_t_kernel(tc, input_vecs, qk_w, sqk, cos, sin, out_0, o
         for it in range(NG + 1):
             s_new = (it + 3) // 2 if it % 2 == 1 and (it + 3) // 2 < NS else None
             if it >= 1:
-                add_t(it - 1, 0)
-            if it + 1 < NG:
-                mx_half(it + 1, 0, REPS)
-            if it >= 1:
-                add_t(it - 1, 1)
+                add_t(it - 1)
             if s_new is not None:
                 x_tp(s_new)
             if it < NG:
@@ -258,7 +256,7 @@ def tile_attentionhead_pa_t_kernel(tc, input_vecs, qk_w, sqk, cos, sin, out_0, o
             if it % 2 == 0 and (it + 2) // 2 < NS:
                 x_q((it + 2) // 2)
             if it + 1 < NG:
-                mx_half(it + 1, 1, REPS)
+                mx(it + 1, DUP)
             if it >= 1:
                 finish(it - 1)
             if s_new is not None and s_new in XE_ON_S:

@@ -19,8 +19,8 @@ NJ = DI // P
 GT = 2 * P
 NS = B * NPAIR
 NG = 2 * NS
-DUP = 0
-XE_ON_S = (1, 9, 13)
+DUP = 3
+XE_ON_S = (1,)
 FLOPS = 2 * B * T * D * 2 * DI
 
 
@@ -79,6 +79,7 @@ def tile_attentionhead_pa_t_kernel(tc, input_vecs, qk_w, sqk, cos, sin, out_0, o
         banks = {}
         prod_tiles = {}
         r_banks = {}
+        norm_tiles = {}
 
         def rows_tp(key, rows):
             pts = []
@@ -191,40 +192,64 @@ def tile_attentionhead_pa_t_kernel(tc, input_vecs, qk_w, sqk, cos, sin, out_0, o
                             stop=True,
                         )
 
-        def sum_squares(g, i, ssq):
+        def sum_squares(g, i):
+            if i == 0:
+                ssq = small.tile([P, 2], F32, tag="ssq", name="ssq")
+                rho = small.tile([P, 2], F32, tag="rho", name="rho")
+                ot = outs.tile([P, 2, DI], F32, tag="ot", name="ot")
+                norm_tiles[g] = (ssq, rho, ot)
             junk = stage.tile([P, DI], BF16, tag="junk", name="junk")
-            nc.scalar.activation(out=junk[:], in_=r_banks[g][i][:], func=ACT.Square, accum_out=ssq[:, i : i + 1])
+            nc.scalar.activation(
+                out=junk[:], in_=r_banks[g][i][:], func=ACT.Square, accum_out=norm_tiles[g][0][:, i : i + 1]
+            )
 
-        def finish(g):
+        def inv_norm(g, i):
+            ssq, rho, ot = norm_tiles[g]
+            col = slice(i, i + 1)
+            nc.scalar.activation(out=rho[:, col], in_=ssq[:, col], func=ACT.Abs_reciprocal_sqrt, scale=1.0 / D)
+
+        def scale_out(g, i):
+            ssq, rho, ot = norm_tiles[g]
+            nc.scalar.activation(out=ot[:, i, :], in_=r_banks[g][i][:], func=ACT.Copy, scale=rho[:, i : i + 1])
+
+        def gain_store(g):
             s, h = divmod(g, 2)
             b, q = divmod(s, NPAIR)
-            ssq = small.tile([P, 2], F32, tag="ssq", name="ssq")
-            rho = small.tile([P, 2], F32, tag="rho", name="rho")
-            ot = outs.tile([P, 2, DI], F32, tag="ot", name="ot")
-            if g == NG - 1:
-                for i in range(2):
-                    col = slice(i, i + 1)
-                    sum_squares(g, i, ssq)
-                    nc.scalar.activation(out=rho[:, col], in_=ssq[:, col], func=ACT.Abs_reciprocal_sqrt, scale=1.0 / D)
-                    nc.vector.scalar_tensor_tensor(
-                        out=ot[:, i, :],
-                        in0=r_banks[g][i][:],
-                        scalar=rho[:, col],
-                        in1=gb[:],
-                        op0=ALU.mult,
-                        op1=ALU.mult,
-                    )
-                    nc.sync.dma_start(out=o_v[h][b][:, 2 * q + i, :], in_=ot[:, i, :])
-                return
-            for i in range(2):
-                sum_squares(g, i, ssq)
-            nc.scalar.activation(out=rho[:], in_=ssq[:], func=ACT.Abs_reciprocal_sqrt, scale=1.0 / D)
-            for i in range(2):
-                nc.scalar.activation(out=ot[:, i, :], in_=r_banks[g][i][:], func=ACT.Copy, scale=rho[:, i : i + 1])
+            ot = norm_tiles[g][2]
             nc.gpsimd.tensor_tensor(
                 out=ot[:], in0=ot[:], in1=gb[:].unsqueeze(1).to_broadcast([P, 2, DI]), op=ALU.mult
             )
             nc.sync.dma_start(out=o_v[h][b][:, 2 * q : 2 * q + 2, :], in_=ot[:])
+
+        def last_unit(g, i):
+            s, h = divmod(g, 2)
+            b, q = divmod(s, NPAIR)
+            ssq, rho, ot = norm_tiles[g]
+            nc.vector.scalar_tensor_tensor(
+                out=ot[:, i, :],
+                in0=r_banks[g][i][:],
+                scalar=rho[:, i : i + 1],
+                in1=gb[:],
+                op0=ALU.mult,
+                op1=ALU.mult,
+            )
+            nc.sync.dma_start(out=o_v[h][b][:, 2 * q + i, :], in_=ot[:, i, :])
+
+        def finish(g):
+            last = g == NG - 1
+            sum_squares(g, 0)
+            if g >= 1:
+                scale_out(g - 1, 1)
+                gain_store(g - 1)
+            inv_norm(g, 0)
+            if last:
+                last_unit(g, 0)
+            sum_squares(g, 1)
+            if not last:
+                scale_out(g, 0)
+            inv_norm(g, 1)
+            if last:
+                last_unit(g, 1)
 
         w_tp(0)
         rows_ev(("w", 0), (False, True))

@@ -21,6 +21,7 @@ NS = B * NPAIR
 NG = 2 * NS
 DUP = 3
 XE_ON_S = (1,)
+SPIN_FIRST = 6
 FLOPS = 2 * B * T * D * 2 * DI
 
 
@@ -50,6 +51,17 @@ def tile_attentionhead_pa_t_kernel(tc, input_vecs, qk_w, sqk, cos, sin, out_0, o
         nc.vector.memset(one[:], 1.0)
         warm = const.tile([P, 1], F32, name="warm")
         nc.scalar.activation(out=warm[:], in_=one[:], func=ACT.Abs_reciprocal_sqrt)
+        zl = const.tile([P, P], BF16, name="zl")
+        nc.vector.memset(zl[:], 0.0)
+        zr = const.tile([P, 2 * GT], BF16, name="zr")
+        nc.vector.memset(zr[:], 0.0)
+        dm = psum_mx.tile([P, 2 * GT], F32, tag="mx", name="dm")
+
+        def spin(n):
+            for rep in range(n):
+                nc.tensor.matmul(out=dm[:], lhsT=zl[:], rhs=zr[:], start=True, stop=True)
+
+        spin(SPIN_FIRST)
 
         xr = [const.tile([P, NT, D], BF16, name="xr%d" % b) for b in range(B)]
         wr = const.tile([P, 2 * NJ, D], BF16, name="wr")
@@ -62,7 +74,8 @@ def tile_attentionhead_pa_t_kernel(tc, input_vecs, qk_w, sqk, cos, sin, out_0, o
         ws = const.tile([P, 2 * DI], U8, name="ws", align_bytes=64)
         tabs = const.tile([P, 2, NJ, NPAIR, GT], BF16, name="tabs")
 
-        nc.sync.dma_start(out=wr[:, 0:NJ, :], in_=w_v[:, 0:NJ, :])
+        nc.sync.dma_start(out=wr[:, 0:2, :], in_=w_v[:, 0:2, :])
+        nc.sync.dma_start(out=wr[:, 2:NJ, :], in_=w_v[:, 2:NJ, :])
         nc.sync.dma_start(out=xr[0][:, 0:2, :], in_=x_v[0][:, 0:2, :])
         nc.sync.dma_start(out=wr[:, NJ : 2 * NJ, :], in_=w_v[:, NJ : 2 * NJ, :])
         for lo, hi in ((0, 2), (2, 4), (4, 8)):
@@ -221,6 +234,13 @@ def tile_attentionhead_pa_t_kernel(tc, input_vecs, qk_w, sqk, cos, sin, out_0, o
             )
             nc.sync.dma_start(out=o_v[h][b][:, 2 * q : 2 * q + 2, :], in_=ot[:])
 
+        def gain_store_unit(g, i):
+            s, h = divmod(g, 2)
+            b, q = divmod(s, NPAIR)
+            ot = norm_tiles[g][2]
+            nc.gpsimd.tensor_tensor(out=ot[:, i, :], in0=ot[:, i, :], in1=gb[:], op=ALU.mult)
+            nc.sync.dma_start(out=o_v[h][b][:, 2 * q + i, :], in_=ot[:, i, :])
+
         def last_unit(g, i):
             s, h = divmod(g, 2)
             b, q = divmod(s, NPAIR)
@@ -238,7 +258,9 @@ def tile_attentionhead_pa_t_kernel(tc, input_vecs, qk_w, sqk, cos, sin, out_0, o
         def finish(g):
             last = g == NG - 1
             sum_squares(g, 0)
-            if g >= 1:
+            if last:
+                last_unit(g - 1, 1)
+            elif g >= 1:
                 scale_out(g - 1, 1)
                 gain_store(g - 1)
             inv_norm(g, 0)
@@ -247,21 +269,27 @@ def tile_attentionhead_pa_t_kernel(tc, input_vecs, qk_w, sqk, cos, sin, out_0, o
             sum_squares(g, 1)
             if not last:
                 scale_out(g, 0)
+            if g == NG - 2:
+                gain_store_unit(g, 0)
             inv_norm(g, 1)
             if last:
                 last_unit(g, 1)
 
         w_tp(0)
+        spin(1)
         rows_ev(("w", 0), (False, True))
         x_tp(0)
         rows_ev(("x", 0), (False,))
         w_q(0)
         x_q(0)
         w_tp(1)
+        spin(1)
         rows_ev(("w", 1), (True, False))
         w_q(1)
         tab(0, False)
+        spin(1)
         tab(0, True)
+        spin(1)
         mx(0, 0)
         x_tp(1)
         rows_ev(("x", 1), (True,))

from contextlib import ExitStack

import concourse.mybir as mybir
from concourse.masks import make_identity

F32 = mybir.dt.float32
BF16 = mybir.dt.bfloat16
U32 = mybir.dt.uint32
U8 = mybir.dt.uint8
FP8X4 = mybir.dt.float8_e4m3fn_x4
ACT = mybir.ActivationFunctionType
ALU = mybir.AluOpType

P = 128
B, T, D, DI = 4, 1024, 512, 512
NT = T // P
NPAIR = NT // 2
NJ = DI // P
GT = 2 * P
NS = B * NPAIR
NG = 2 * NS
DUP = 3
XE_ON_S = (1,)
SPIN_FIRST = 6
FLOPS = 2 * B * T * D * 2 * DI


def tile_attentionhead_pa_t_kernel(tc, input_vecs, qk_w, sqk, cos, sin, out_0, out_1):
    nc = tc.nc
    x_v = input_vecs.rearrange("b (p n) k -> b p n k", n=NT)
    w_v = qk_w.rearrange("(r p) k -> p r k", p=P)
    cos_v = cos.rearrange("(p n) c -> p n c", n=NT)
    sin_v = sin.rearrange("(p n) c -> p n c", n=NT)
    o_v = [o.rearrange("b (p n) c -> b p n c", n=NT) for o in (out_0, out_1)]

    with ExitStack() as ctx:
        const = ctx.enter_context(tc.tile_pool(name="const", bufs=1))
        stage = ctx.enter_context(tc.tile_pool(name="stage", bufs=3))
        prods = ctx.enter_context(tc.tile_pool(name="prods", bufs=6))
        outs = ctx.enter_context(tc.tile_pool(name="outs", bufs=4))
        small = ctx.enter_context(tc.tile_pool(name="small", bufs=4))
        psum_mx = ctx.enter_context(tc.psum_pool(name="psum_mx", bufs=3))
        psum_tp = ctx.enter_context(tc.psum_pool(name="psum_tp", bufs=5))
        ctx.enter_context(tc.manual_schedule())

        ident_f = const.tile([P, P], F32, name="ident_f")
        make_identity(nc, ident_f[:])
        ident_b = const.tile([P, P], BF16, name="ident_b")
        make_identity(nc, ident_b[:])
        one = const.tile([P, 1], F32, name="one")
        nc.vector.memset(one[:], 1.0)
        warm = const.tile([P, 1], F32, name="warm")
        nc.scalar.activation(out=warm[:], in_=one[:], func=ACT.Abs_reciprocal_sqrt)
        zl = const.tile([P, P], BF16, name="zl")
        nc.vector.memset(zl[:], 0.0)
        zr = const.tile([P, 2 * GT], BF16, name="zr")
        nc.vector.memset(zr[:], 0.0)
        dm = psum_mx.tile([P, 2 * GT], F32, tag="mx", name="dm")

        def spin(n):
            for rep in range(n):
                nc.tensor.matmul(out=dm[:], lhsT=zl[:], rhs=zr[:], start=True, stop=True)

        spin(SPIN_FIRST)

        xr = [const.tile([P, NT, D], BF16, name="xr%d" % b) for b in range(B)]
        wr = const.tile([P, 2 * NJ, D], BF16, name="wr")
        cr = const.tile([P, NT, DI], BF16, name="cr")
        sr = const.tile([P, NT, DI], BF16, name="sr")
        gb = const.tile([P, DI], BF16, name="gb")
        xc = const.tile([P, B * T], U32, name="xc", align_bytes=64)
        xs = const.tile([P, B * T], U8, name="xs", align_bytes=64)
        wc = const.tile([P, 2 * DI], U32, name="wc", align_bytes=64)
        ws = const.tile([P, 2 * DI], U8, name="ws", align_bytes=64)
        tabs = const.tile([P, 2, NJ, NPAIR, GT], BF16, name="tabs")

        nc.sync.dma_start(out=wr[:, 0:2, :], in_=w_v[:, 0:2, :])
        nc.sync.dma_start(out=wr[:, 2:NJ, :], in_=w_v[:, 2:NJ, :])
        nc.sync.dma_start(out=xr[0][:, 0:2, :], in_=x_v[0][:, 0:2, :])
        nc.sync.dma_start(out=wr[:, NJ : 2 * NJ, :], in_=w_v[:, NJ : 2 * NJ, :])
        for lo, hi in ((0, 2), (2, 4), (4, 8)):
            if lo > 0:
                nc.sync.dma_start(out=xr[0][:, lo:hi, :], in_=x_v[0][:, lo:hi, :])
            nc.sync.dma_start(out=cr[:, lo:hi, :], in_=cos_v[:, lo:hi, :])
            nc.sync.dma_start(out=sr[:, lo:hi, :], in_=sin_v[:, lo:hi, :])
        nc.sync.dma_start(out=gb[:], in_=sqk.partition_broadcast(P))
        for b in range(1, B):
            nc.sync.dma_start(out=xr[b][:], in_=x_v[b])

        grouped = {}
        word_banks = {}
        banks = {}
        prod_tiles = {}
        r_banks = {}
        norm_tiles = {}

        def rows_tp(key, rows):
            pts = []
            for m in range(len(rows) // 2):
                pt = psum_tp.tile([P, 2, 2, P], F32, tag="tp", name="pt")
                pts.append(pt)
                for i in range(2):
                    words = rows[2 * m + i].bitcast(F32)
                    for u in range(2):
                        nc.tensor.transpose(pt[:, i, u, :], words[:, u * P : (u + 1) * P], ident_f[:])
            word_banks[key] = pts

        def rows_ev(key, on_scalar):
            pts = word_banks[key]
            g_t = stage.tile([P, len(pts) * 2 * P * 4], BF16, tag="g%d" % len(pts), name="g_t", align_bytes=64)
            grouped[key] = g_t
            gw = g_t[:].bitcast(F32).rearrange("p (m i r u) -> p m i r u", i=2, r=P, u=2)
            for m in range(len(pts)):
                src = pts[m][:].rearrange("p i u r -> p i r u")
                if on_scalar[m]:
                    nc.scalar.copy(out=gw[:, m], in_=src)
                else:
                    nc.vector.tensor_copy(out=gw[:, m], in_=src)

        def w_tp(h):
            rows_tp(("w", h), [wr[:, h * NJ + j, :] for j in range(NJ)])

        def w_q(h):
            cols = slice(h * DI, (h + 1) * DI)
            nc.vector.quantize_mx(out=wc[:, cols].bitcast(FP8X4), scales=ws[:, cols], in_=grouped[("w", h)][:])

        def x_tp(s):
            b, q = divmod(s, NPAIR)
            rows_tp(("x", s), [xr[b][:, 2 * q + i, :] for i in range(2)])

        def x_q(s):
            cols = slice(s * GT, (s + 1) * GT)
            nc.vector.quantize_mx(out=xc[:, cols].bitcast(FP8X4), scales=xs[:, cols], in_=grouped[("x", s)][:])

        def tab(q, is_sin):
            raw = sr if is_sin else cr
            ptb = psum_tp.tile([P, NJ, GT], BF16, tag="tp", name="ptb")
            for j in range(NJ):
                for i in range(2):
                    nc.tensor.transpose(
                        ptb[:, j, i * P : (i + 1) * P], raw[:, 2 * q + i, j * P : (j + 1) * P], ident_b[:]
                    )
            if is_sin:
                nc.scalar.copy(out=tabs[:, 1, 0:2, q, :], in_=ptb[:, 2:4, :])
                nc.scalar.mul(out=tabs[:, 1, 2:4, q, :], in_=ptb[:, 0:2, :], mul=-1.0)
            else:
                nc.scalar.copy(out=tabs[:, 0, :, q, :], in_=ptb[:])

        def mx(g, dup):
            s, h = divmod(g, 2)
            tok = slice(s * GT, (s + 1) * GT)
            banks[g] = []
            for pr in range(2):
                x2 = psum_mx.tile([P, 2, GT], F32, tag="mx", name="x2")
                banks[g].append(x2)
                for t2 in range(2):
                    c0 = h * DI + (pr + 2 * t2) * P
                    for rep in range(2 if 2 * pr + t2 < dup else 1):
                        nc.tensor.matmul_mx(
                            out=x2[:, t2, :],
                            lhsT=wc[:, c0 : c0 + P].bitcast(FP8X4),
                            lhsT_scale=ws[:, c0 : c0 + P],
                            rhs=xc[:, tok].bitcast(FP8X4),
                            rhs_scale=xs[:, tok],
                            start=True,
                            stop=True,
                        )

        def prod(g, pr):
            q = (g // 2) % NPAIR
            ab = prods.tile([P, 2, 2, GT], F32, tag="ab", name="ab")
            prod_tiles[(g, pr)] = ab
            nc.vector.tensor_tensor(
                out=ab[:],
                in0=banks[g][pr][:].unsqueeze(1).to_broadcast([P, 2, 2, GT]),
                in1=tabs[:, :, slice(pr, NJ, 2), q, :],
                op=ALU.mult,
            )

        def add_t(g):
            r_banks[g] = []
            for i in range(2):
                rb = psum_tp.tile([P, DI], F32, tag="tp", name="rb")
                r_banks[g].append(rb)
                ts = slice(i * P, (i + 1) * P)
                for pr in range(2):
                    ab = prod_tiles[(g, pr)]
                    for t2 in range(2):
                        j = pr + 2 * t2
                        cs = slice(j * P, (j + 1) * P)
                        nc.tensor.matmul(
                            out=rb[:, cs],
                            lhsT=ab[:, 0, t2, ts],
                            rhs=ident_f[:],
                            is_transpose=True,
                            start=True,
                            stop=False,
                        )
                        nc.tensor.matmul(
                            out=rb[:, cs],
                            lhsT=ab[:, 1, 1 - t2, ts],
                            rhs=ident_f[:],
                            is_transpose=True,
                            start=False,
                            stop=True,
                        )

        def sum_squares(g, i):
            if i == 0:
                ssq = small.tile([P, 2], F32, tag="ssq", name="ssq")
                rho = small.tile([P, 2], F32, tag="rho", name="rho")
                ot = outs.tile([P, 2, DI], F32, tag="ot", name="ot")
                norm_tiles[g] = (ssq, rho, ot)
            junk = stage.tile([P, DI], BF16, tag="junk", name="junk")
            nc.scalar.activation(
                out=junk[:], in_=r_banks[g][i][:], func=ACT.Square, accum_out=norm_tiles[g][0][:, i : i + 1]
            )

        def inv_norm(g, i):
            ssq, rho, ot = norm_tiles[g]
            col = slice(i, i + 1)
            nc.scalar.activation(out=rho[:, col], in_=ssq[:, col], func=ACT.Abs_reciprocal_sqrt, scale=1.0 / D)

        def scale_out(g, i):
            ssq, rho, ot = norm_tiles[g]
            nc.scalar.activation(out=ot[:, i, :], in_=r_banks[g][i][:], func=ACT.Copy, scale=rho[:, i : i + 1])

        def gain_store(g):
            s, h = divmod(g, 2)
            b, q = divmod(s, NPAIR)
            ot = norm_tiles[g][2]
            nc.gpsimd.tensor_tensor(
                out=ot[:], in0=ot[:], in1=gb[:].unsqueeze(1).to_broadcast([P, 2, DI]), op=ALU.mult
            )
            nc.sync.dma_start(out=o_v[h][b][:, 2 * q : 2 * q + 2, :], in_=ot[:])

        def gain_store_unit(g, i):
            s, h = divmod(g, 2)
            b, q = divmod(s, NPAIR)
            ot = norm_tiles[g][2]
            nc.gpsimd.tensor_tensor(out=ot[:, i, :], in0=ot[:, i, :], in1=gb[:], op=ALU.mult)
            nc.sync.dma_start(out=o_v[h][b][:, 2 * q + i, :], in_=ot[:, i, :])

        def last_unit(g, i):
            s, h = divmod(g, 2)
            b, q = divmod(s, NPAIR)
            ssq, rho, ot = norm_tiles[g]
            nc.vector.scalar_tensor_tensor(
                out=ot[:, i, :],
                in0=r_banks[g][i][:],
                scalar=rho[:, i : i + 1],
                in1=gb[:],
                op0=ALU.mult,
                op1=ALU.mult,
            )
            nc.sync.dma_start(out=o_v[h][b][:, 2 * q + i, :], in_=ot[:, i, :])

        def finish(g):
            last = g == NG - 1
            sum_squares(g, 0)
            if last:
                last_unit(g - 1, 1)
            elif g >= 1:
                scale_out(g - 1, 1)
                gain_store(g - 1)
            inv_norm(g, 0)
            if last:
                last_unit(g, 0)
            sum_squares(g, 1)
            if not last:
                scale_out(g, 0)
            if g == NG - 2:
                gain_store_unit(g, 0)
            inv_norm(g, 1)
            if last:
                last_unit(g, 1)

        w_tp(0)
        spin(1)
        rows_ev(("w", 0), (False, True))
        x_tp(0)
        rows_ev(("x", 0), (False,))
        w_q(0)
        x_q(0)
        w_tp(1)
        spin(1)
        rows_ev(("w", 1), (True, False))
        w_q(1)
        tab(0, False)
        spin(1)
        tab(0, True)
        spin(1)
        mx(0, 0)
        x_tp(1)
        rows_ev(("x", 1), (True,))

        tab_at = {0: ((1, False), (1, True)), 1: ((2, False),), 2: ((2, True),), 3: ((3, False),), 4: ((3, True),)}
        for it in range(NG + 1):
            s_new = (it + 3) // 2 if it % 2 == 1 and (it + 3) // 2 < NS else None
            if it >= 1:
                add_t(it - 1)
            if s_new is not None:
                x_tp(s_new)
            if it < NG:
                prod(it, 0)
                prod(it, 1)
            if s_new is not None and s_new not in XE_ON_S:
                rows_ev(("x", s_new), (False,))
            if it % 2 == 0 and (it + 2) // 2 < NS:
                x_q((it + 2) // 2)
            if it + 1 < NG:
                mx(it + 1, DUP)
            if it >= 1:
                finish(it - 1)
            if s_new is not None and s_new in XE_ON_S:
                rows_ev(("x", s_new), (True,))
            for q, is_sin in tab_at.get(it, ()):
                tab(q, is_sin)
